import numpy as np
import ml_dtypes


BF16 = ml_dtypes.bfloat16


def bf(x):
    return np.asarray(x, np.float32).astype(BF16)


def f64(x):
    return np.asarray(x).astype(np.float64)


E2M1 = np.array([0.0, 0.5, 1.0, 1.5, 2.0, 3.0, 4.0, 6.0, -0.0, -0.5, -1.0, -1.5, -2.0, -3.0, -4.0, -6.0])


def pack_weight(w, fmt):
    k, n = w.shape
    w = f64(bf(w)).reshape(k // 32, 32, n)
    amax = np.abs(w).max(1)
    if fmt == "e4m3":
        byte = np.frexp(amax)[1] - 1 + 127 - 7
    else:
        mant, ex = np.frexp(amax / 6.0)
        byte = np.where(mant > 0.5, ex, ex - 1) + 127
    byte = np.clip(np.where(amax > 0, byte, 1), 1, 254)
    scaled = (w * np.exp2(127.0 - byte)[:, None, :]).reshape(k, n).astype(np.float32)
    by_word = np.ascontiguousarray(scaled.reshape(k // 512, 128, 4, n).transpose(0, 1, 3, 2))
    if fmt == "e4m3":
        words = by_word.astype(ml_dtypes.float8_e4m3fn).view(np.uint8)
    else:
        c = by_word.astype(ml_dtypes.float4_e2m1fn).view(np.uint8) & 0xF
        words = c[..., 0::2] | (c[..., 1::2] << 4)
    return np.ascontiguousarray(words), np.ascontiguousarray(byte.astype(np.uint8).reshape(k // 512, 16, n))


def unpack_weight(words, scales, fmt):
    g, p, n, _ = words.shape
    if fmt == "e4m3":
        vals = np.ascontiguousarray(words).view(ml_dtypes.float8_e4m3fn).astype(np.float64)
    else:
        nib = np.empty((g, p, n, 4), np.uint8)
        nib[..., 0::2] = words & 0xF
        nib[..., 1::2] = words >> 4
        vals = E2M1[nib]
    vals = vals * np.repeat(np.exp2(scales.astype(np.float64) - 127.0), 8, axis=1)[..., None]
    return vals.transpose(0, 1, 3, 2).reshape(g * 512, n)

def pack4(w):
    words, scales = pack_weight(w, "e2m1")
    return words.reshape(words.shape[0], 128, -1), scales


def unpack4(words, scales):
    return unpack_weight(words.reshape(words.shape[0], 128, -1, 2), scales, "e2m1")


def kspread(k):
    return np.exp2(np.repeat(np.random.randint(-6, 7, k // 32), 32).astype(np.float64))


B, L, K, D, H = 4, 128, 4096, 512, 2
DH = D // H
RD = D // 2
HALF = RD // 2
ROPE_BASE = 10000.0


def apply_rope(t):
    pos = np.arange(L, dtype=np.float64)[:, None]
    inv = np.exp(np.arange(0, RD, 2, dtype=np.float64) * (-np.log(ROPE_BASE) / RD))
    theta = pos * inv
    cos, sin = np.cos(theta), np.sin(theta)
    t1, t2 = t[..., :HALF], t[..., HALF:RD]
    return np.concatenate([t1 * cos - t2 * sin, t1 * sin + t2 * cos], axis=-1)


def split_heads(t):
    return t.reshape(B, L, H, DH).transpose(0, 2, 1, 3)


def setup_inputs():
    s = kspread(K)
    x = np.random.standard_normal((B, L, K)) * s
    x_words, x_scales = pack4(np.ascontiguousarray(x.reshape(B * L, K).T))
    w = np.random.standard_normal((3 * D, K)) / np.sqrt(K) / s[None, :]
    words, scales = pack4(np.ascontiguousarray(w.T))
    b = bf(np.random.standard_normal(3 * D) * 0.3)
    return {"x_words": x_words,
            "x_scales": x_scales,
            "Wqkv_w_words": words,
            "Wqkv_w_scales": scales,
            "Wqkv_b": b}


def reference(x_words, x_scales, Wqkv_w_words, Wqkv_w_scales, Wqkv_b):
    xq = unpack4(x_words, x_scales).T.reshape(B, L, K)
    qkv = (xq @ unpack4(Wqkv_w_words, Wqkv_w_scales)) + f64(Wqkv_b)
    q, k, v = np.split(qkv, 3, axis=-1)
    q, k, v = split_heads(q), split_heads(k), split_heads(v)
    return apply_rope(q), apply_rope(k), v

@@ -1,0 +1,232 @@
+from contextlib import ExitStack
+import math
+
+import concourse.mybir as mybir
+
+FLOPS = 2 * 512 * 4096 * 1536
+
+F32 = mybir.dt.float32
+BF16 = mybir.dt.bfloat16
+I32 = mybir.dt.int32
+U8 = mybir.dt.uint8
+FP4X4 = mybir.dt.float4_e2m1fn_x4
+ALU = mybir.AluOpType
+ACTF = mybir.ActivationFunctionType
+
+P = 128
+PASSES = 8
+BLOCKS = 4
+COLS = 512
+HALF = 128
+ROPE_BASE = 10000.0
+N_WARM = 6
+
+CHUNKS_FIRST = [(0, 1), (1, 2), (2, 4), (4, 6), (6, 8)]
+CHUNKS_LATER = [(0, 2), (2, 4), (4, 6), (6, 8)]
+GPSIMD_ADDS = True
+
+
+def tile_ropeattention_pa_kernel(tc, x_words, x_scales, w_words, w_scales, w_bias, out_q, out_k, out_v):
+    nc = tc.nc
+    with ExitStack() as ctx:
+        keep = ctx.enter_context(tc.tile_pool(name="keep", bufs=1))
+        work = ctx.enter_context(tc.tile_pool(name="work", bufs=2))
+        outs = ctx.enter_context(tc.tile_pool(name="outs", bufs=4))
+        psum = ctx.enter_context(tc.psum_pool(name="psum", bufs=8))
+        ctx.enter_context(tc.manual_schedule())
+
+        warm = keep.tile([P, COLS], BF16, name="warm")
+        nc.gpsimd.memset(warm[:].bitcast(F32), 0.0)
+        brow = keep.tile([P, 3 * COLS], BF16, name="brow")
+        nc.gpsimd.memset(brow[:].bitcast(F32), 0.0)
+        nc.gpsimd.dma_start(out=brow[0:1, :], in_=w_bias.rearrange("(o n) -> o n", o=1))
+        ones = keep.tile([P, P], BF16, name="ones")
+        nc.gpsimd.memset(ones[:], 1.0)
+        pos = keep.tile([P, 1], F32, name="pos")
+        nc.gpsimd.iota(pos[:], pattern=[[0, 1]], base=0, channel_multiplier=1, allow_small_or_imprecise_dtypes=True)
+
+        scr = keep.tile([P, 1], F32, name="scr")
+        nc.scalar.activation(out=scr[:], in_=warm[:, 0:1], func=ACTF.Sin)
+
+        xs = keep.tile([P, PASSES, COLS], U8, name="xs", align_bytes=64)
+        nc.vector.memset(xs[:].bitcast(I32), 0)
+        plane_runs = {0: [(0, 2), (2, 8)], 1: [(0, 8)], 2: [(0, 8)]}
+        w_plane = {}
+        plane_tiles = {}
+        for c in range(3):
+            for (g0, g1) in plane_runs[c]:
+                pt = keep.tile([P, g1 - g0, COLS], U8, name="ws%d_%d" % (c, g0), align_bytes=64)
+                plane_tiles[(c, g0)] = pt
+                if c == 0:
+                    nc.vector.memset(pt[:].bitcast(I32), 0)
+                else:
+                    nc.gpsimd.memset(pt[:].bitcast(F32), 0.0)
+                for g in range(g0, g1):
+                    w_plane[(c, g)] = (pt, g - g0)
+
+        def load_planes(pt, src, g0, g1, c0):
+            for quad in range(4):
+                nc.sync.dma_start(
+                    out=pt[32 * quad : 32 * quad + 4, :, :].bitcast(I32),
+                    in_=src[g0:g1, 4 * quad : 4 * quad + 4, c0 : c0 + COLS].rearrange("g r n -> r g n").bitcast(I32),
+                )
+
+        x_code = {}
+        w_code = {}
+
+        def load_x(g0, g1):
+            t = keep.tile([P, g1 - g0, 2 * COLS], U8, name="xc%d" % g0, align_bytes=64)
+            nc.sync.dma_start(out=t[:].bitcast(I32), in_=x_words[g0:g1].rearrange("g p n -> p g n").bitcast(I32))
+            for g in range(g0, g1):
+                x_code[g] = (t, g - g0)
+
+        def load_w(c, g0, g1):
+            t = keep.tile([P, g1 - g0, 2 * COLS], U8, name="wc%d_%d" % (c, g0), align_bytes=64)
+            nc.sync.dma_start(
+                out=t[:].bitcast(I32),
+                in_=w_words[g0:g1, :, 2 * COLS * c : 2 * COLS * (c + 1)].rearrange("g p n -> p g n").bitcast(I32),
+            )
+            for g in range(g0, g1):
+                w_code[(c, g)] = (t, g - g0)
+
+        load_x(0, 1)
+        load_w(0, 0, 1)
+        load_planes(xs, x_scales, 0, PASSES, 0)
+        load_planes(plane_tiles[(0, 0)], w_scales, 0, 2, 0)
+        load_x(1, 2)
+        load_w(0, 1, 2)
+        load_planes(plane_tiles[(0, 2)], w_scales, 2, 8, 0)
+        for (g0, g1) in CHUNKS_FIRST[2:]:
+            load_x(g0, g1)
+            load_w(0, g0, g1)
+        for c in (1, 2):
+            load_planes(plane_tiles[(c, 0)], w_scales, 0, PASSES, COLS * c)
+            for (g0, g1) in CHUNKS_LATER:
+                load_w(c, g0, g1)
+
+        inv = keep.tile([P, HALF], F32, name="inv")
+        nc.vector.memset(inv[:, 0:1], 1.0)
+        for s in range(7):
+            w = 2 ** s
+            nc.vector.tensor_scalar(
+                out=inv[:, w : 2 * w], in0=inv[:, 0:w], scalar1=ROPE_BASE ** (-w / 128.0), scalar2=None, op0=ALU.mult
+            )
+        turn = keep.tile([P, 1], F32, name="turn")
+        nc.vector.tensor_scalar(out=turn[:], in0=pos[:], scalar1=1.0 / (2.0 * math.pi), scalar2=None, op0=ALU.mult)
+        ang = keep.tile([P, 2, HALF], F32, name="ang")
+        nc.vector.tensor_scalar(out=ang[:, 0, :], in0=inv[:], scalar1=turn[:, 0:1], scalar2=None, op0=ALU.mult)
+        nc.vector.tensor_scalar(
+            out=ang[:, 1, :], in0=inv[:], scalar1=turn[:, 0:1], scalar2=0.25, op0=ALU.mult, op1=ALU.add
+        )
+        whole = keep.tile([P, 2, HALF], I32, name="whole")
+        nc.vector.tensor_copy(out=whole[:], in_=ang[:])
+        frac = keep.tile([P, 2, HALF], F32, name="frac")
+        nc.vector.tensor_tensor(out=frac[:], in0=ang[:], in1=whole[:], op=ALU.subtract)
+        nfr = keep.tile([P, 2, HALF], F32, name="nfr")
+        nc.vector.scalar_tensor_tensor(
+            out=nfr[:].rearrange("p a d -> p (a d)"),
+            in0=frac[:].rearrange("p a d -> p (a d)"),
+            scalar=0.5,
+            in1=frac[:].rearrange("p a d -> p (a d)"),
+            op0=ALU.is_gt,
+            op1=ALU.subtract,
+        )
+        tab = keep.tile([P, 2, 2, HALF], F32, name="tab")
+        for h in range(2):
+            nc.scalar.activation(out=tab[:, :, h, :], in_=nfr[:], func=ACTF.Sin, scale=-2.0 * math.pi)
+        sin2 = tab[:, 0, :, :]
+        cos2 = tab[:, 1, :, :]
+
+        def rotate(src, dst):
+            s4 = src.rearrange("p (h t d) -> p h t d", h=2, t=2)
+            d4 = dst.rearrange("p (h t d) -> p h t d", h=2, t=2)
+            mc = work.tile([P, 2, 2, HALF], F32, name="mc", tag="mc")
+            ms = work.tile([P, 2, 2, HALF], F32, name="ms", tag="ms")
+            nc.vector.tensor_tensor(out=ms[:, :, 1, :], in0=s4[:, :, 1, :], in1=sin2, op=ALU.mult)
+            nc.vector.tensor_tensor(out=mc[:, :, 0, :], in0=s4[:, :, 0, :], in1=cos2, op=ALU.mult)
+            nc.vector.tensor_tensor(out=ms[:, :, 0, :], in0=s4[:, :, 0, :], in1=sin2, op=ALU.mult)
+            nc.vector.tensor_tensor(out=mc[:, :, 1, :], in0=s4[:, :, 1, :], in1=cos2, op=ALU.mult)
+            nc.vector.tensor_tensor(out=d4[:, :, 0, :], in0=mc[:, :, 0, :], in1=ms[:, :, 1, :], op=ALU.subtract)
+            nc.vector.tensor_tensor(out=d4[:, :, 1, :], in0=mc[:, :, 1, :], in1=ms[:, :, 0, :], op=ALU.add)
+
+        def mx_pass(acc, c, i, g, n0, n1):
+            xt, xl = x_code[g]
+            wt, wl = w_code[(c, g)]
+            st, sl = w_plane[(c, g)]
+            nc.tensor.matmul_mx(
+                out=acc,
+                lhsT=xt[:, xl, 2 * P * i : 2 * P * (i + 1)].bitcast(FP4X4),
+                lhsT_scale=xs[:, g, P * i : P * (i + 1)],
+                rhs=wt[:, wl, 2 * n0 : 2 * n1].bitcast(FP4X4),
+                rhs_scale=st[:, sl, n0:n1],
+                start=(g == 0),
+                stop=(g == PASSES - 1),
+            )
+
+        warm_ps = psum.tile([P, COLS], F32, name="warm_ps", tag="acc")
+        for n in range(N_WARM):
+            nc.tensor.matmul(out=warm_ps[:], lhsT=warm[:, 0:P], rhs=warm[:], start=True, stop=True)
+
+        acc_q = []
+        for i in range(BLOCKS):
+            acc_i = psum.tile([P, COLS], F32, name="acc_q%d" % i, tag="acc")
+            acc_q.append(acc_i)
+        for g in range(2):
+            for i in range(BLOCKS):
+                mx_pass(acc_q[i][:], 0, i, g, 0, COLS)
+
+        bias_ps = []
+        for c in range(3):
+            b_ps = psum.tile([P, COLS], F32, name="bias_ps%d" % c, tag="acc")
+            nc.tensor.matmul(out=b_ps[:], lhsT=ones[:], rhs=brow[:, COLS * c : COLS * (c + 1)], start=True, stop=True)
+            bias_ps.append(b_ps)
+        bias_v = keep.tile([P, COLS], F32, name="bias_v")
+        nc.scalar.copy(out=bias_v[:], in_=bias_ps[2][:])
+        bias_rot = []
+        for c in range(2):
+            br = keep.tile([P, COLS], F32, name="bias_rot%d" % c)
+            rotate(bias_ps[c][:], br[:])
+            bias_rot.append(br)
+
+        for g in range(2, PASSES):
+            for i in range(BLOCKS):
+                mx_pass(acc_q[i][:], 0, i, g, 0, COLS)
+
+        def finish_rope(acc, c, i, dst):
+            rot = work.tile([P, COLS], F32, name="rot", tag="rot")
+            rotate(acc[:], rot[:])
+            o = outs.tile([P, COLS], F32, name="o", tag="o")
+            if GPSIMD_ADDS:
+                nc.gpsimd.tensor_tensor(out=o[:], in0=rot[:], in1=bias_rot[c][:], op=ALU.add)
+            else:
+                nc.vector.tensor_tensor(out=o[:], in0=rot[:], in1=bias_rot[c][:], op=ALU.add)
+            nc.scalar.dma_start(out=dst[i].rearrange("h l d -> l h d"), in_=o[:].rearrange("p (h e) -> p h e", h=2))
+
+        for i in range(BLOCKS):
+            finish_rope(acc_q[i], 0, i, out_q)
+
+        for i in range(BLOCKS):
+            acc = psum.tile([P, COLS], F32, name="acc_k%d" % i, tag="acc")
+            for g in range(PASSES):
+                mx_pass(acc[:], 1, i, g, 0, COLS)
+            finish_rope(acc, 1, i, out_k)
+
+        for i in range(BLOCKS - 1):
+            acc = psum.tile([P, COLS], F32, name="acc_v%d" % i, tag="acc")
+            for g in range(PASSES):
+                mx_pass(acc[:], 2, i, g, 0, COLS)
+            o = outs.tile([P, COLS], F32, name="o", tag="o")
+            nc.vector.tensor_tensor(out=o[:], in0=acc[:], in1=bias_v[:], op=ALU.add)
+            nc.scalar.dma_start(out=out_v[i].rearrange("h l d -> l h d"), in_=o[:].rearrange("p (h e) -> p h e", h=2))
+
+        i = BLOCKS - 1
+        for h in range(2):
+            acc = psum.tile([P, COLS // 2], F32, name="acc_v3%d" % h, tag="acc")
+            for g in range(PASSES):
+                mx_pass(acc[:], 2, i, g, 256 * h, 256 * (h + 1))
+            o = outs.tile([P, COLS], F32, name="o", tag="o")
+            nc.vector.tensor_tensor(out=o[:, 0:256], in0=acc[:], in1=bias_v[:, 256 * h : 256 * (h + 1)], op=ALU.add)
+            if h == 0:
+                nc.sync.dma_start(out=out_v[i, h], in_=o[:, 0:256])
+            else:
+                nc.scalar.dma_start(out=out_v[i, h], in_=o[:, 0:256])

@@ -19,60 +19,53 @@ BLOCKS = 4
 COLS = 512
 HALF = 128
 ROPE_BASE = 10000.0
-N_WARM = 6
-
-CHUNKS_FIRST = [(0, 1), (1, 2), (2, 4), (4, 6), (6, 8)]
-CHUNKS_LATER = [(0, 2), (2, 4), (4, 6), (6, 8)]
-GPSIMD_ADDS = True
+WARM = 5
+SPLIT = 3
 
 
 def tile_ropeattention_pa_kernel(tc, x_words, x_scales, w_words, w_scales, w_bias, out_q, out_k, out_v):
     nc = tc.nc
     with ExitStack() as ctx:
         keep = ctx.enter_context(tc.tile_pool(name="keep", bufs=1))
-        work = ctx.enter_context(tc.tile_pool(name="work", bufs=2))
-        outs = ctx.enter_context(tc.tile_pool(name="outs", bufs=4))
-        psum = ctx.enter_context(tc.psum_pool(name="psum", bufs=8))
+        work = ctx.enter_context(tc.tile_pool(name="work", bufs=3))
+        psum = ctx.enter_context(tc.psum_pool(name="psum", bufs=1))
         ctx.enter_context(tc.manual_schedule())
 
-        warm = keep.tile([P, COLS], BF16, name="warm")
-        nc.gpsimd.memset(warm[:].bitcast(F32), 0.0)
+        x_code = {}
+        w_code = {}
+        w_plane = {}
+
+        def bank(n, name, width):
+            return psum.tile([P, width], F32, name=name, tag="bank%d" % n)
+
+        def new_planes(name, g0, g1, width):
+            pt = keep.tile([P, g1 - g0, width], U8, name=name, align_bytes=64)
+            nc.vector.memset(pt[:].bitcast(I32), 0)
+            return pt
+
         brow = keep.tile([P, 3 * COLS], BF16, name="brow")
         nc.gpsimd.memset(brow[:].bitcast(F32), 0.0)
         nc.gpsimd.dma_start(out=brow[0:1, :], in_=w_bias.rearrange("(o n) -> o n", o=1))
-        ones = keep.tile([P, P], BF16, name="ones")
-        nc.gpsimd.memset(ones[:], 1.0)
         pos = keep.tile([P, 1], F32, name="pos")
         nc.gpsimd.iota(pos[:], pattern=[[0, 1]], base=0, channel_multiplier=1, allow_small_or_imprecise_dtypes=True)
+
+        warm = keep.tile([P, COLS], BF16, name="warm")
+        nc.vector.memset(warm[:].bitcast(I32), 0)
+        xs = new_planes("xs", 0, PASSES, COLS)
+        qks_a = new_planes("qks_a", 0, SPLIT, 2 * COLS)
+        ones = keep.tile([P, P], BF16, name="ones")
+        nc.vector.memset(ones[:], 1.0)
+        qs_b = new_planes("qs_b", SPLIT, PASSES, COLS)
 
         scr = keep.tile([P, 1], F32, name="scr")
         nc.scalar.activation(out=scr[:], in_=warm[:, 0:1], func=ACTF.Sin)
 
-        xs = keep.tile([P, PASSES, COLS], U8, name="xs", align_bytes=64)
-        nc.vector.memset(xs[:].bitcast(I32), 0)
-        plane_runs = {0: [(0, 2), (2, 8)], 1: [(0, 8)], 2: [(0, 8)]}
-        w_plane = {}
-        plane_tiles = {}
-        for c in range(3):
-            for (g0, g1) in plane_runs[c]:
-                pt = keep.tile([P, g1 - g0, COLS], U8, name="ws%d_%d" % (c, g0), align_bytes=64)
-                plane_tiles[(c, g0)] = pt
-                if c == 0:
-                    nc.vector.memset(pt[:].bitcast(I32), 0)
-                else:
-                    nc.gpsimd.memset(pt[:].bitcast(F32), 0.0)
-                for g in range(g0, g1):
-                    w_plane[(c, g)] = (pt, g - g0)
-
-        def load_planes(pt, src, g0, g1, c0):
-            for quad in range(4):
+        def load_planes(pt, src, g0, g1, c0, width):
+            for r in range(4):
                 nc.sync.dma_start(
-                    out=pt[32 * quad : 32 * quad + 4, :, :].bitcast(I32),
-                    in_=src[g0:g1, 4 * quad : 4 * quad + 4, c0 : c0 + COLS].rearrange("g r n -> r g n").bitcast(I32),
+                    out=pt[r : P : 32, :, :].bitcast(I32),
+                    in_=src[g0:g1, r : 16 : 4, c0 : c0 + width].rearrange("g q n -> q g n").bitcast(I32),
                 )
-
-        x_code = {}
-        w_code = {}
 
         def load_x(g0, g1):
             t = keep.tile([P, g1 - g0, 2 * COLS], U8, name="xc%d" % g0, align_bytes=64)
@@ -80,49 +73,59 @@ def tile_ropeattention_pa_kernel(tc, x_words, x_scales, w_words, w_scales, w_bia
             for g in range(g0, g1):
                 x_code[g] = (t, g - g0)
 
-        def load_w(c, g0, g1):
-            t = keep.tile([P, g1 - g0, 2 * COLS], U8, name="wc%d_%d" % (c, g0), align_bytes=64)
+        def load_w(c0, c1, g0, g1):
+            t = keep.tile([P, g1 - g0, 2 * COLS * (c1 - c0)], U8, name="wc%d_%d" % (c0, g0), align_bytes=64)
             nc.sync.dma_start(
                 out=t[:].bitcast(I32),
-                in_=w_words[g0:g1, :, 2 * COLS * c : 2 * COLS * (c + 1)].rearrange("g p n -> p g n").bitcast(I32),
+                in_=w_words[g0:g1, :, 2 * COLS * c0 : 2 * COLS * c1].rearrange("g p n -> p g n").bitcast(I32),
             )
-            for g in range(g0, g1):
-                w_code[(c, g)] = (t, g - g0)
+            for c in range(c0, c1):
+                for g in range(g0, g1):
+                    w_code[(c, g)] = (t, g - g0, COLS * (c - c0))
+
+        def note_planes(pt, c0, c1, g0, g1):
+            for c in range(c0, c1):
+                for g in range(g0, g1):
+                    w_plane[(c, g)] = (pt, g - g0, COLS * (c - c0))
 
         load_x(0, 1)
-        load_w(0, 0, 1)
-        load_planes(xs, x_scales, 0, PASSES, 0)
-        load_planes(plane_tiles[(0, 0)], w_scales, 0, 2, 0)
-        load_x(1, 2)
-        load_w(0, 1, 2)
-        load_planes(plane_tiles[(0, 2)], w_scales, 2, 8, 0)
-        for (g0, g1) in CHUNKS_FIRST[2:]:
-            load_x(g0, g1)
-            load_w(0, g0, g1)
-        for c in (1, 2):
-            load_planes(plane_tiles[(c, 0)], w_scales, 0, PASSES, COLS * c)
-            for (g0, g1) in CHUNKS_LATER:
-                load_w(c, g0, g1)
+        load_w(0, 1, 0, 1)
+        load_planes(xs, x_scales, 0, PASSES, 0, COLS)
+        load_planes(qks_a, w_scales, 0, SPLIT, 0, 2 * COLS)
+        note_planes(qks_a, 0, 2, 0, SPLIT)
+        load_w(1, 2, 0, 1)
+        load_x(1, 3)
+        load_w(0, 2, 1, 2)
+        load_w(0, 2, 2, 3)
+        load_planes(qs_b, w_scales, SPLIT, PASSES, 0, COLS)
+        note_planes(qs_b, 0, 1, SPLIT, PASSES)
+        load_x(3, 5)
+        load_w(0, 1, 3, 5)
+        load_x(5, 8)
+        load_w(0, 1, 5, 8)
 
         inv = keep.tile([P, HALF], F32, name="inv")
         nc.vector.memset(inv[:, 0:1], 1.0)
+        turn = keep.tile([P, 1], F32, name="turn")
+        nc.vector.tensor_scalar(out=turn[:], in0=pos[:], scalar1=1.0 / (2.0 * math.pi), scalar2=None, op0=ALU.mult)
         for s in range(7):
             w = 2 ** s
             nc.vector.tensor_scalar(
                 out=inv[:, w : 2 * w], in0=inv[:, 0:w], scalar1=ROPE_BASE ** (-w / 128.0), scalar2=None, op0=ALU.mult
             )
-        turn = keep.tile([P, 1], F32, name="turn")
-        nc.vector.tensor_scalar(out=turn[:], in0=pos[:], scalar1=1.0 / (2.0 * math.pi), scalar2=None, op0=ALU.mult)
-        ang = keep.tile([P, 2, HALF], F32, name="ang")
-        nc.vector.tensor_scalar(out=ang[:, 0, :], in0=inv[:], scalar1=turn[:, 0:1], scalar2=None, op0=ALU.mult)
-        nc.vector.tensor_scalar(
-            out=ang[:, 1, :], in0=inv[:], scalar1=turn[:, 0:1], scalar2=0.25, op0=ALU.mult, op1=ALU.add
-        )
-        whole = keep.tile([P, 2, HALF], I32, name="whole")
+        ang = keep.tile([P, 4, HALF], F32, name="ang")
+        for a in range(4):
+            if a < 2:
+                nc.vector.tensor_scalar(out=ang[:, a, :], in0=inv[:], scalar1=turn[:, 0:1], scalar2=None, op0=ALU.mult)
+            else:
+                nc.vector.tensor_scalar(
+                    out=ang[:, a, :], in0=inv[:], scalar1=turn[:, 0:1], scalar2=0.25, op0=ALU.mult, op1=ALU.add
+                )
+        whole = keep.tile([P, 4, HALF], I32, name="whole")
         nc.vector.tensor_copy(out=whole[:], in_=ang[:])
-        frac = keep.tile([P, 2, HALF], F32, name="frac")
+        frac = keep.tile([P, 4, HALF], F32, name="frac")
         nc.vector.tensor_tensor(out=frac[:], in0=ang[:], in1=whole[:], op=ALU.subtract)
-        nfr = keep.tile([P, 2, HALF], F32, name="nfr")
+        nfr = keep.tile([P, 4, HALF], F32, name="nfr")
         nc.vector.scalar_tensor_tensor(
             out=nfr[:].rearrange("p a d -> p (a d)"),
             in0=frac[:].rearrange("p a d -> p (a d)"),
@@ -131,102 +134,117 @@ def tile_ropeattention_pa_kernel(tc, x_words, x_scales, w_words, w_scales, w_bia
             op0=ALU.is_gt,
             op1=ALU.subtract,
         )
-        tab = keep.tile([P, 2, 2, HALF], F32, name="tab")
-        for h in range(2):
-            nc.scalar.activation(out=tab[:, :, h, :], in_=nfr[:], func=ACTF.Sin, scale=-2.0 * math.pi)
-        sin2 = tab[:, 0, :, :]
-        cos2 = tab[:, 1, :, :]
+        arg = keep.tile([P, 2, 2, HALF], F32, name="arg")
+        nc.vector.tensor_copy(out=arg[:, 1, :, :], in_=nfr[:, 2:4, :])
+        nc.vector.tensor_copy(out=arg[:, 0, 0, :], in_=nfr[:, 0, :])
+        nc.vector.tensor_scalar(out=arg[:, 0, 1, :], in0=nfr[:, 1, :], scalar1=-1.0, scalar2=None, op0=ALU.mult)
+        ks_b = new_planes("ks_b", SPLIT, PASSES, COLS)
+        vs = new_planes("vs", 0, PASSES, COLS)
 
-        def rotate(src, dst):
-            s4 = src.rearrange("p (h t d) -> p h t d", h=2, t=2)
-            d4 = dst.rearrange("p (h t d) -> p h t d", h=2, t=2)
-            mc = work.tile([P, 2, 2, HALF], F32, name="mc", tag="mc")
-            ms = work.tile([P, 2, 2, HALF], F32, name="ms", tag="ms")
-            nc.vector.tensor_tensor(out=ms[:, :, 1, :], in0=s4[:, :, 1, :], in1=sin2, op=ALU.mult)
-            nc.vector.tensor_tensor(out=mc[:, :, 0, :], in0=s4[:, :, 0, :], in1=cos2, op=ALU.mult)
-            nc.vector.tensor_tensor(out=ms[:, :, 0, :], in0=s4[:, :, 0, :], in1=sin2, op=ALU.mult)
-            nc.vector.tensor_tensor(out=mc[:, :, 1, :], in0=s4[:, :, 1, :], in1=cos2, op=ALU.mult)
-            nc.vector.tensor_tensor(out=d4[:, :, 0, :], in0=mc[:, :, 0, :], in1=ms[:, :, 1, :], op=ALU.subtract)
-            nc.vector.tensor_tensor(out=d4[:, :, 1, :], in0=mc[:, :, 1, :], in1=ms[:, :, 0, :], op=ALU.add)
+        load_planes(ks_b, w_scales, SPLIT, PASSES, COLS, COLS)
+        note_planes(ks_b, 1, 2, SPLIT, PASSES)
+        load_w(1, 2, 3, 8)
+        load_planes(vs, w_scales, 0, PASSES, 2 * COLS, COLS)
+        note_planes(vs, 2, 3, 0, PASSES)
+        load_w(2, 3, 0, 4)
+        load_w(2, 3, 4, 8)
+
+        warm_ps = bank(4, "warm_ps", COLS)
+        for n in range(WARM):
+            nc.tensor.matmul(out=warm_ps[:], lhsT=warm[:, 0:P], rhs=warm[:], start=True, stop=True)
+        bias_sb = keep.tile([P, 3 * COLS], F32, name="bias_sb")
+        for c in range(3):
+            b_ps = bank(5 + c, "bias_ps%d" % c, COLS)
+            nc.tensor.matmul(out=b_ps[:], lhsT=ones[:], rhs=brow[:, COLS * c : COLS * (c + 1)], start=True, stop=True)
+            nc.scalar.copy(out=bias_sb[:, COLS * c : COLS * (c + 1)], in_=b_ps[:])
+
+        tab = keep.tile([P, 2, 2, 2, HALF], F32, name="tab")
+        for h in range(2):
+            nc.scalar.activation(out=tab[:, :, h, :, :], in_=arg[:], func=ACTF.Sin, scale=-2.0 * math.pi)
+        sin4 = tab[:, 0, :, :, :].rearrange("p h t d -> p (h t d)")
+        cos4 = tab[:, 1, :, :, :].rearrange("p h t d -> p (h t d)")
+
+        def products(eng, src, tag):
+            mc = work.tile([P, COLS], F32, name="mc" + tag, tag="mc" + tag)
+            ms = work.tile([P, COLS], F32, name="ms" + tag, tag="ms" + tag)
+            eng.tensor_tensor(out=mc[:], in0=src, in1=cos4, op=ALU.mult)
+            eng.tensor_tensor(out=ms[:], in0=src, in1=sin4, op=ALU.mult)
+            return mc, ms
+
+        def combine(eng, pair, dst):
+            mc, ms = pair
+            eng.tensor_tensor(
+                out=dst.rearrange("p (h t d) -> p h t d", h=2, t=2),
+                in0=mc[:].rearrange("p (h t d) -> p h t d", h=2, t=2),
+                in1=ms[:].rearrange("p (h t d) -> p h t d", h=2, t=2)[:, :, ::-1, :],
+                op=ALU.add,
+            )
+
+        bias_rot = keep.tile([P, 2 * COLS], F32, name="bias_rot")
+        combine(nc.gpsimd, products(nc.gpsimd, bias_sb[:, 0:COLS], "g"), bias_rot[:, 0:COLS])
+        combine(nc.vector, products(nc.vector, bias_sb[:, COLS : 2 * COLS], ""), bias_rot[:, COLS : 2 * COLS])
 
         def mx_pass(acc, c, i, g, n0, n1):
             xt, xl = x_code[g]
-            wt, wl = w_code[(c, g)]
-            st, sl = w_plane[(c, g)]
+            wt, wl, wo = w_code[(c, g)]
+            st, sl, so = w_plane[(c, g)]
             nc.tensor.matmul_mx(
                 out=acc,
                 lhsT=xt[:, xl, 2 * P * i : 2 * P * (i + 1)].bitcast(FP4X4),
                 lhsT_scale=xs[:, g, P * i : P * (i + 1)],
-                rhs=wt[:, wl, 2 * n0 : 2 * n1].bitcast(FP4X4),
-                rhs_scale=st[:, sl, n0:n1],
+                rhs=wt[:, wl, 2 * (wo + n0) : 2 * (wo + n1)].bitcast(FP4X4),
+                rhs_scale=st[:, sl, so + n0 : so + n1],
                 start=(g == 0),
                 stop=(g == PASSES - 1),
             )
 
-        warm_ps = psum.tile([P, COLS], F32, name="warm_ps", tag="acc")
-        for n in range(N_WARM):
-            nc.tensor.matmul(out=warm_ps[:], lhsT=warm[:, 0:P], rhs=warm[:], start=True, stop=True)
+        first = [(c, i) for c in range(2) for i in range(BLOCKS)]
+        acc_of = {}
+        for (c, i) in first:
+            acc_of[(c, i)] = bank(4 * c + i, "acc%d_%d" % (c, i), COLS)
+        for g in range(SPLIT):
+            for (c, i) in first:
+                mx_pass(acc_of[(c, i)][:], c, i, g, 0, COLS)
 
-        acc_q = []
-        for i in range(BLOCKS):
-            acc_i = psum.tile([P, COLS], F32, name="acc_q%d" % i, tag="acc")
-            acc_q.append(acc_i)
-        for g in range(2):
-            for i in range(BLOCKS):
-                mx_pass(acc_q[i][:], 0, i, g, 0, COLS)
+        dst_of = {0: out_q, 1: out_k}
+        bias_v = bias_sb[:, 2 * COLS : 3 * COLS]
 
-        bias_ps = []
-        for c in range(3):
-            b_ps = psum.tile([P, COLS], F32, name="bias_ps%d" % c, tag="acc")
-            nc.tensor.matmul(out=b_ps[:], lhsT=ones[:], rhs=brow[:, COLS * c : COLS * (c + 1)], start=True, stop=True)
-            bias_ps.append(b_ps)
-        bias_v = keep.tile([P, COLS], F32, name="bias_v")
-        nc.scalar.copy(out=bias_v[:], in_=bias_ps[2][:])
-        bias_rot = []
-        for c in range(2):
-            br = keep.tile([P, COLS], F32, name="bias_rot%d" % c)
-            rotate(bias_ps[c][:], br[:])
-            bias_rot.append(br)
+        def finish(n, pair):
+            c, i = first[n]
+            rot = keep.tile([P, COLS], F32, name="rot%d" % n)
+            combine(nc.vector, pair, rot[:])
+            o = keep.tile([P, COLS], F32, name="o_rope%d" % n)
+            nc.gpsimd.tensor_tensor(out=o[:], in0=rot[:], in1=bias_rot[:, COLS * c : COLS * (c + 1)], op=ALU.add)
+            nc.sync.dma_start(
+                out=dst_of[c][i].rearrange("h l d -> l h d"), in_=o[:].rearrange("p (h e) -> p h e", h=2)
+            )
 
-        for g in range(2, PASSES):
-            for i in range(BLOCKS):
-                mx_pass(acc_q[i][:], 0, i, g, 0, COLS)
-
-        def finish_rope(acc, c, i, dst):
-            rot = work.tile([P, COLS], F32, name="rot", tag="rot")
-            rotate(acc[:], rot[:])
-            o = outs.tile([P, COLS], F32, name="o", tag="o")
-            if GPSIMD_ADDS:
-                nc.gpsimd.tensor_tensor(out=o[:], in0=rot[:], in1=bias_rot[c][:], op=ALU.add)
-            else:
-                nc.vector.tensor_tensor(out=o[:], in0=rot[:], in1=bias_rot[c][:], op=ALU.add)
-            nc.scalar.dma_start(out=dst[i].rearrange("h l d -> l h d"), in_=o[:].rearrange("p (h e) -> p h e", h=2))
-
-        for i in range(BLOCKS):
-            finish_rope(acc_q[i], 0, i, out_q)
-
-        for i in range(BLOCKS):
-            acc = psum.tile([P, COLS], F32, name="acc_k%d" % i, tag="acc")
-            for g in range(PASSES):
-                mx_pass(acc[:], 1, i, g, 0, COLS)
-            finish_rope(acc, 1, i, out_k)
+        held = None
+        for n, (c, i) in enumerate(first):
+            for g in range(SPLIT, PASSES):
+                mx_pass(acc_of[(c, i)][:], c, i, g, 0, COLS)
+            pair = products(nc.vector, acc_of[(c, i)][:], "")
+            if n > 0:
+                finish(n - 1, held)
+            held = pair
+        finish(len(first) - 1, held)
 
         for i in range(BLOCKS - 1):
-            acc = psum.tile([P, COLS], F32, name="acc_v%d" % i, tag="acc")
+            acc = bank(i, "acc2_%d" % i, COLS)
             for g in range(PASSES):
                 mx_pass(acc[:], 2, i, g, 0, COLS)
-            o = outs.tile([P, COLS], F32, name="o", tag="o")
-            nc.vector.tensor_tensor(out=o[:], in0=acc[:], in1=bias_v[:], op=ALU.add)
+            o = keep.tile([P, COLS], F32, name="o_v%d" % i)
+            nc.vector.tensor_tensor(out=o[:], in0=acc[:], in1=bias_v, op=ALU.add)
             nc.scalar.dma_start(out=out_v[i].rearrange("h l d -> l h d"), in_=o[:].rearrange("p (h e) -> p h e", h=2))
 
         i = BLOCKS - 1
         for h in range(2):
-            acc = psum.tile([P, COLS // 2], F32, name="acc_v3%d" % h, tag="acc")
+            acc = bank(3 + h, "acc2_3%d" % h, COLS // 2)
             for g in range(PASSES):
                 mx_pass(acc[:], 2, i, g, 256 * h, 256 * (h + 1))
-            o = outs.tile([P, COLS], F32, name="o", tag="o")
-            nc.vector.tensor_tensor(out=o[:, 0:256], in0=acc[:], in1=bias_v[:, 256 * h : 256 * (h + 1)], op=ALU.add)
+            o = keep.tile([P, COLS // 2], F32, name="o_v3%d" % h)
+            nc.vector.tensor_tensor(out=o[:], in0=acc[:], in1=bias_v[:, 256 * h : 256 * (h + 1)], op=ALU.add)
             if h == 0:
-                nc.sync.dma_start(out=out_v[i, h], in_=o[:, 0:256])
+                nc.sync.dma_start(out=out_v[i, h], in_=o[:])
             else:
-                nc.scalar.dma_start(out=out_v[i, h], in_=o[:, 0:256])
+                nc.scalar.dma_start(out=out_v[i, h], in_=o[:])

@@ -19,8 +19,8 @@ BLOCKS = 4
 COLS = 512
 HALF = 128
 ROPE_BASE = 10000.0
-WARM = 5
-SPLIT = 3
+WARM = 4
+SPLIT = 4
 
 
 def tile_ropeattention_pa_kernel(tc, x_words, x_scales, w_words, w_scales, w_bias, out_q, out_k, out_v):
@@ -43,19 +43,26 @@ def tile_ropeattention_pa_kernel(tc, x_words, x_scales, w_words, w_scales, w_bia
             nc.vector.memset(pt[:].bitcast(I32), 0)
             return pt
 
-        brow = keep.tile([P, 3 * COLS], BF16, name="brow")
-        nc.gpsimd.memset(brow[:].bitcast(F32), 0.0)
-        nc.gpsimd.dma_start(out=brow[0:1, :], in_=w_bias.rearrange("(o n) -> o n", o=1))
+        brow = keep.tile([P, 768], BF16, name="brow")
+        nc.vector.memset(brow[:].bitcast(I32), 0)
+        nc.scalar.dma_start(out=brow[0:P:64, :], in_=w_bias.rearrange("(a n) -> a n", a=2))
+        sel = keep.tile([P, 2, P], BF16, name="sel")
+        nc.gpsimd.memset(sel[:].bitcast(F32), 0.0)
+        nc.gpsimd.memset(sel[0:1, 0, :], 1.0)
+        nc.gpsimd.memset(sel[64:65, 1, :], 1.0)
         pos = keep.tile([P, 1], F32, name="pos")
         nc.gpsimd.iota(pos[:], pattern=[[0, 1]], base=0, channel_multiplier=1, allow_small_or_imprecise_dtypes=True)
 
         warm = keep.tile([P, COLS], BF16, name="warm")
         nc.vector.memset(warm[:].bitcast(I32), 0)
-        xs = new_planes("xs", 0, PASSES, COLS)
-        qks_a = new_planes("qks_a", 0, SPLIT, 2 * COLS)
-        ones = keep.tile([P, P], BF16, name="ones")
-        nc.vector.memset(ones[:], 1.0)
-        qs_b = new_planes("qs_b", SPLIT, PASSES, COLS)
+        xs_a = new_planes("xs_a", 0, 3, COLS)
+        qks_a = new_planes("qks_a", 0, 2, 2 * COLS)
+        qks_b = new_planes("qks_b", 2, SPLIT, 2 * COLS)
+        xs_b = new_planes("xs_b", 3, PASSES, COLS)
+        qs_c = new_planes("qs_c", SPLIT, PASSES, COLS)
+        x_plane = {}
+        for g in range(PASSES):
+            x_plane[g] = (xs_a, g) if g < 3 else (xs_b, g - 3)
 
         scr = keep.tile([P, 1], F32, name="scr")
         nc.scalar.activation(out=scr[:], in_=warm[:, 0:1], func=ACTF.Sin)
@@ -90,19 +97,24 @@ def tile_ropeattention_pa_kernel(tc, x_words, x_scales, w_words, w_scales, w_bia
 
         load_x(0, 1)
         load_w(0, 1, 0, 1)
-        load_planes(xs, x_scales, 0, PASSES, 0, COLS)
-        load_planes(qks_a, w_scales, 0, SPLIT, 0, 2 * COLS)
-        note_planes(qks_a, 0, 2, 0, SPLIT)
+        load_planes(xs_a, x_scales, 0, 3, 0, COLS)
+        load_planes(qks_a, w_scales, 0, 2, 0, 2 * COLS)
+        note_planes(qks_a, 0, 2, 0, 2)
         load_w(1, 2, 0, 1)
-        load_x(1, 3)
+        load_x(1, 2)
         load_w(0, 2, 1, 2)
+        load_planes(qks_b, w_scales, 2, SPLIT, 0, 2 * COLS)
+        note_planes(qks_b, 0, 2, 2, SPLIT)
+        load_x(2, 3)
         load_w(0, 2, 2, 3)
-        load_planes(qs_b, w_scales, SPLIT, PASSES, 0, COLS)
-        note_planes(qs_b, 0, 1, SPLIT, PASSES)
-        load_x(3, 5)
-        load_w(0, 1, 3, 5)
-        load_x(5, 8)
-        load_w(0, 1, 5, 8)
+        load_planes(xs_b, x_scales, 3, PASSES, 0, COLS)
+        load_x(3, 4)
+        load_w(0, 2, 3, 4)
+        load_planes(qs_c, w_scales, SPLIT, PASSES, 0, COLS)
+        note_planes(qs_c, 0, 1, SPLIT, PASSES)
+        for g in range(SPLIT, PASSES):
+            load_x(g, g + 1)
+            load_w(0, 1, g, g + 1)
 
         inv = keep.tile([P, HALF], F32, name="inv")
         nc.vector.memset(inv[:, 0:1], 1.0)
@@ -143,7 +155,7 @@ def tile_ropeattention_pa_kernel(tc, x_words, x_scales, w_words, w_scales, w_bia
 
         load_planes(ks_b, w_scales, SPLIT, PASSES, COLS, COLS)
         note_planes(ks_b, 1, 2, SPLIT, PASSES)
-        load_w(1, 2, 3, 8)
+        load_w(1, 2, SPLIT, PASSES)
         load_planes(vs, w_scales, 0, PASSES, 2 * COLS, COLS)
         note_planes(vs, 2, 3, 0, PASSES)
         load_w(2, 3, 0, 4)
@@ -153,9 +165,17 @@ def tile_ropeattention_pa_kernel(tc, x_words, x_scales, w_words, w_scales, w_bia
         for n in range(WARM):
             nc.tensor.matmul(out=warm_ps[:], lhsT=warm[:, 0:P], rhs=warm[:], start=True, stop=True)
         bias_sb = keep.tile([P, 3 * COLS], F32, name="bias_sb")
+        pieces = {0: [(0, 0, 0, 512)], 1: [(0, 512, 0, 256), (1, 0, 256, 256)], 2: [(1, 256, 0, 512)]}
         for c in range(3):
             b_ps = bank(5 + c, "bias_ps%d" % c, COLS)
-            nc.tensor.matmul(out=b_ps[:], lhsT=ones[:], rhs=brow[:, COLS * c : COLS * (c + 1)], start=True, stop=True)
+            for (row, src0, dst0, width) in pieces[c]:
+                nc.tensor.matmul(
+                    out=b_ps[:, dst0 : dst0 + width],
+                    lhsT=sel[:, row, :],
+                    rhs=brow[:, src0 : src0 + width],
+                    start=True,
+                    stop=True,
+                )
             nc.scalar.copy(out=bias_sb[:, COLS * c : COLS * (c + 1)], in_=b_ps[:])
 
         tab = keep.tile([P, 2, 2, 2, HALF], F32, name="tab")
@@ -186,12 +206,13 @@ def tile_ropeattention_pa_kernel(tc, x_words, x_scales, w_words, w_scales, w_bia
 
         def mx_pass(acc, c, i, g, n0, n1):
             xt, xl = x_code[g]
+            xp, xpl = x_plane[g]
             wt, wl, wo = w_code[(c, g)]
             st, sl, so = w_plane[(c, g)]
             nc.tensor.matmul_mx(
                 out=acc,
                 lhsT=xt[:, xl, 2 * P * i : 2 * P * (i + 1)].bitcast(FP4X4),
-                lhsT_scale=xs[:, g, P * i : P * (i + 1)],
+                lhsT_scale=xp[:, xpl, P * i : P * (i + 1)],
                 rhs=wt[:, wl, 2 * (wo + n0) : 2 * (wo + n1)].bitcast(FP4X4),
                 rhs_scale=st[:, sl, so + n0 : so + n1],
                 start=(g == 0),

@@ -20,7 +20,7 @@ COLS = 512
 HALF = 128
 ROPE_BASE = 10000.0
 WARM = 4
-SPLIT = 4
+SPLIT = 3
 
 
 def tile_ropeattention_pa_kernel(tc, x_words, x_scales, w_words, w_scales, w_bias, out_q, out_k, out_v):
@@ -55,14 +55,13 @@ def tile_ropeattention_pa_kernel(tc, x_words, x_scales, w_words, w_scales, w_bia
 
         warm = keep.tile([P, COLS], BF16, name="warm")
         nc.vector.memset(warm[:].bitcast(I32), 0)
-        xs_a = new_planes("xs_a", 0, 3, COLS)
-        qks_a = new_planes("qks_a", 0, 2, 2 * COLS)
-        qks_b = new_planes("qks_b", 2, SPLIT, 2 * COLS)
-        xs_b = new_planes("xs_b", 3, PASSES, COLS)
+        xs_a = new_planes("xs_a", 0, 4, COLS)
+        qks_a = new_planes("qks_a", 0, SPLIT, 2 * COLS)
         qs_c = new_planes("qs_c", SPLIT, PASSES, COLS)
+        xs_b = new_planes("xs_b", 4, PASSES, COLS)
         x_plane = {}
         for g in range(PASSES):
-            x_plane[g] = (xs_a, g) if g < 3 else (xs_b, g - 3)
+            x_plane[g] = (xs_a, g) if g < 4 else (xs_b, g - 4)
 
         scr = keep.tile([P, 1], F32, name="scr")
         nc.scalar.activation(out=scr[:], in_=warm[:, 0:1], func=ACTF.Sin)
@@ -97,24 +96,20 @@ def tile_ropeattention_pa_kernel(tc, x_words, x_scales, w_words, w_scales, w_bia
 
         load_x(0, 1)
         load_w(0, 1, 0, 1)
-        load_planes(xs_a, x_scales, 0, 3, 0, COLS)
-        load_planes(qks_a, w_scales, 0, 2, 0, 2 * COLS)
-        note_planes(qks_a, 0, 2, 0, 2)
+        load_planes(xs_a, x_scales, 0, 4, 0, COLS)
+        load_planes(qks_a, w_scales, 0, SPLIT, 0, 2 * COLS)
+        note_planes(qks_a, 0, 2, 0, SPLIT)
         load_w(1, 2, 0, 1)
         load_x(1, 2)
         load_w(0, 2, 1, 2)
-        load_planes(qks_b, w_scales, 2, SPLIT, 0, 2 * COLS)
-        note_planes(qks_b, 0, 2, 2, SPLIT)
-        load_x(2, 3)
-        load_w(0, 2, 2, 3)
-        load_planes(xs_b, x_scales, 3, PASSES, 0, COLS)
-        load_x(3, 4)
-        load_w(0, 2, 3, 4)
         load_planes(qs_c, w_scales, SPLIT, PASSES, 0, COLS)
         note_planes(qs_c, 0, 1, SPLIT, PASSES)
-        for g in range(SPLIT, PASSES):
-            load_x(g, g + 1)
-            load_w(0, 1, g, g + 1)
+        load_x(2, 3)
+        load_w(0, 2, 2, 3)
+        load_planes(xs_b, x_scales, 4, PASSES, 0, COLS)
+        for (g0, g1) in ((3, 5), (5, 7), (7, 8)):
+            load_x(g0, g1)
+            load_w(0, 1, g0, g1)
 
         inv = keep.tile([P, HALF], F32, name="inv")
         nc.vector.memset(inv[:, 0:1], 1.0)

@@ -225,15 +225,23 @@ def tile_ropeattention_pa_kernel(tc, x_words, x_scales, w_words, w_scales, w_bia
         dst_of = {0: out_q, 1: out_k}
         bias_v = bias_sb[:, 2 * COLS : 3 * COLS]
 
-        def finish(n, pair):
+        def add_on_gpsimd(name, src, addend, dst):
+            o = keep.tile([P, COLS], F32, name=name)
+            nc.gpsimd.tensor_tensor(out=o[:], in0=src, in1=addend, op=ALU.add)
+            nc.sync.dma_start(out=dst.rearrange("h l d -> l h d"), in_=o[:].rearrange("p (h e) -> p h e", h=2))
+
+        rots = {}
+
+        def bias_rope(n):
             c, i = first[n]
+            add_on_gpsimd("o_rope%d" % n, rots[n][:], bias_rot[:, COLS * c : COLS * (c + 1)], dst_of[c][i])
+
+        def finish(n, pair):
             rot = keep.tile([P, COLS], F32, name="rot%d" % n)
             combine(nc.vector, pair, rot[:])
-            o = keep.tile([P, COLS], F32, name="o_rope%d" % n)
-            nc.gpsimd.tensor_tensor(out=o[:], in0=rot[:], in1=bias_rot[:, COLS * c : COLS * (c + 1)], op=ALU.add)
-            nc.sync.dma_start(
-                out=dst_of[c][i].rearrange("h l d -> l h d"), in_=o[:].rearrange("p (h e) -> p h e", h=2)
-            )
+            rots[n] = rot
+            if n < 5:
+                bias_rope(n)
 
         held = None
         for n, (c, i) in enumerate(first):
@@ -245,7 +253,16 @@ def tile_ropeattention_pa_kernel(tc, x_words, x_scales, w_words, w_scales, w_bia
             held = pair
         finish(len(first) - 1, held)
 
-        for i in range(BLOCKS - 1):
+        acc = bank(0, "acc2_0", COLS)
+        for g in range(PASSES):
+            mx_pass(acc[:], 2, 0, g, 0, COLS)
+        vcp = keep.tile([P, COLS], F32, name="vcp")
+        nc.scalar.copy(out=vcp[:], in_=acc[:])
+        add_on_gpsimd("o_v0", vcp[:], bias_v, out_v[0])
+        for n in range(5, 8):
+            bias_rope(n)
+
+        for i in (1, 2):
             acc = bank(i, "acc2_%d" % i, COLS)
             for g in range(PASSES):
                 mx_pass(acc[:], 2, i, g, 0, COLS)

@@ -184,14 +184,24 @@ def tile_ropeattention_pa_kernel(tc, x_words, x_scales, w_words, w_scales, w_bia
             ms = work.tile([P, COLS], F32, name="ms" + tag, tag="ms" + tag)
             eng.tensor_tensor(out=mc[:], in0=src, in1=cos4, op=ALU.mult)
             eng.tensor_tensor(out=ms[:], in0=src, in1=sin4, op=ALU.mult)
-            return mc, ms
+            return mc[:], ms[:]
+
+        def both_products(src):
+            m = work.tile([P, 2, COLS], F32, name="m2", tag="m2")
+            nc.vector.tensor_tensor(
+                out=m[:],
+                in0=src.unsqueeze(1).to_broadcast([P, 2, COLS]),
+                in1=tab[:].rearrange("p s h t d -> p s (h t d)"),
+                op=ALU.mult,
+            )
+            return m[:, 1, :], m[:, 0, :]
 
         def combine(eng, pair, dst):
             mc, ms = pair
             eng.tensor_tensor(
                 out=dst.rearrange("p (h t d) -> p h t d", h=2, t=2),
-                in0=mc[:].rearrange("p (h t d) -> p h t d", h=2, t=2),
-                in1=ms[:].rearrange("p (h t d) -> p h t d", h=2, t=2)[:, :, ::-1, :],
+                in0=mc.rearrange("p (h t d) -> p h t d", h=2, t=2),
+                in1=ms.rearrange("p (h t d) -> p h t d", h=2, t=2)[:, :, ::-1, :],
                 op=ALU.add,
             )
 
@@ -247,7 +257,7 @@ def tile_ropeattention_pa_kernel(tc, x_words, x_scales, w_words, w_scales, w_bia
         for n, (c, i) in enumerate(first):
             for g in range(SPLIT, PASSES):
                 mx_pass(acc_of[(c, i)][:], c, i, g, 0, COLS)
-            pair = products(nc.vector, acc_of[(c, i)][:], "")
+            pair = both_products(acc_of[(c, i)][:])
             if n > 0:
                 finish(n - 1, held)
             held = pair

@@ -21,13 +21,14 @@ HALF = 128
 ROPE_BASE = 10000.0
 WARM = 4
 SPLIT = 3
+GROUP = 2
 
 
 def tile_ropeattention_pa_kernel(tc, x_words, x_scales, w_words, w_scales, w_bias, out_q, out_k, out_v):
     nc = tc.nc
     with ExitStack() as ctx:
         keep = ctx.enter_context(tc.tile_pool(name="keep", bufs=1))
-        work = ctx.enter_context(tc.tile_pool(name="work", bufs=3))
+        work = ctx.enter_context(tc.tile_pool(name="work", bufs=4))
         psum = ctx.enter_context(tc.psum_pool(name="psum", bufs=1))
         ctx.enter_context(tc.manual_schedule())
 
@@ -250,35 +251,32 @@ def tile_ropeattention_pa_kernel(tc, x_words, x_scales, w_words, w_scales, w_bia
             rot = keep.tile([P, COLS], F32, name="rot%d" % n)
             combine(nc.vector, pair, rot[:])
             rots[n] = rot
-            if n < 5:
-                bias_rope(n)
-
-        held = None
-        for n, (c, i) in enumerate(first):
-            for g in range(SPLIT, PASSES):
-                mx_pass(acc_of[(c, i)][:], c, i, g, 0, COLS)
-            pair = both_products(acc_of[(c, i)][:])
-            if n > 0:
-                finish(n - 1, held)
-            held = pair
-        finish(len(first) - 1, held)
-
-        acc = bank(0, "acc2_0", COLS)
-        for g in range(PASSES):
-            mx_pass(acc[:], 2, 0, g, 0, COLS)
-        vcp = keep.tile([P, COLS], F32, name="vcp")
-        nc.scalar.copy(out=vcp[:], in_=acc[:])
-        add_on_gpsimd("o_v0", vcp[:], bias_v, out_v[0])
-        for n in range(5, 8):
             bias_rope(n)
 
-        for i in (1, 2):
+        def v_tile(i):
             acc = bank(i, "acc2_%d" % i, COLS)
             for g in range(PASSES):
                 mx_pass(acc[:], 2, i, g, 0, COLS)
             o = keep.tile([P, COLS], F32, name="o_v%d" % i)
             nc.vector.tensor_tensor(out=o[:], in0=acc[:], in1=bias_v, op=ALU.add)
             nc.scalar.dma_start(out=out_v[i].rearrange("h l d -> l h d"), in_=o[:].rearrange("p (h e) -> p h e", h=2))
+
+        for n0 in range(0, len(first), GROUP):
+            group = range(n0, n0 + GROUP)
+            for g in range(SPLIT, PASSES):
+                for n in group:
+                    c, i = first[n]
+                    mx_pass(acc_of[(c, i)][:], c, i, g, 0, COLS)
+            held = {}
+            for n in group:
+                held[n] = both_products(acc_of[first[n]][:])
+            if n0 + GROUP == len(first):
+                v_tile(0)
+            for n in group:
+                finish(n, held[n])
+
+        for i in (1, 2):
+            v_tile(i)
 
         i = BLOCKS - 1
         for h in range(2):
@@ -287,7 +285,4 @@ def tile_ropeattention_pa_kernel(tc, x_words, x_scales, w_words, w_scales, w_bia
                 mx_pass(acc[:], 2, i, g, 256 * h, 256 * (h + 1))
             o = keep.tile([P, COLS // 2], F32, name="o_v3%d" % h)
             nc.vector.tensor_tensor(out=o[:], in0=acc[:], in1=bias_v[:, 256 * h : 256 * (h + 1)], op=ALU.add)
-            if h == 0:
-                nc.sync.dma_start(out=out_v[i, h], in_=o[:])
-            else:
-                nc.scalar.dma_start(out=out_v[i, h], in_=o[:])
+            nc.scalar.dma_start(out=out_v[i, h], in_=o[:])

@@ -251,7 +251,8 @@ def tile_ropeattention_pa_kernel(tc, x_words, x_scales, w_words, w_scales, w_bia
             rot = keep.tile([P, COLS], F32, name="rot%d" % n)
             combine(nc.vector, pair, rot[:])
             rots[n] = rot
-            bias_rope(n)
+            if n < len(first) - 1:
+                bias_rope(n)
 
         def v_tile(i):
             acc = bank(i, "acc2_%d" % i, COLS)
@@ -277,6 +278,10 @@ def tile_ropeattention_pa_kernel(tc, x_words, x_scales, w_words, w_scales, w_bia
 
         for i in (1, 2):
             v_tile(i)
+        c7, i7 = first[-1]
+        o7 = keep.tile([P, COLS], F32, name="o_rope7")
+        nc.vector.tensor_tensor(out=o7[:], in0=rots[7][:], in1=bias_rot[:, COLS * c7 : COLS * (c7 + 1)], op=ALU.add)
+        nc.sync.dma_start(out=dst_of[c7][i7].rearrange("h l d -> l h d"), in_=o7[:].rearrange("p (h e) -> p h e", h=2))
 
         i = BLOCKS - 1
         for h in range(2):

@@ -40,7 +40,7 @@ def tile_ropeattention_pa_kernel(tc, x_words, x_scales, w_words, w_scales, w_bia
             return psum.tile([P, width], F32, name=name, tag="bank%d" % n)
 
         def new_planes(name, g0, g1, width):
-            pt = keep.tile([P, g1 - g0, width], U8, name=name, align_bytes=64)
+            pt = keep.tile([P, g1 - g0, width], U8, name=name, align_bytes=256)
             nc.vector.memset(pt[:].bitcast(I32), 0)
             return pt
 
@@ -75,13 +75,13 @@ def tile_ropeattention_pa_kernel(tc, x_words, x_scales, w_words, w_scales, w_bia
                 )
 
         def load_x(g0, g1):
-            t = keep.tile([P, g1 - g0, 2 * COLS], U8, name="xc%d" % g0, align_bytes=64)
+            t = keep.tile([P, g1 - g0, 2 * COLS], U8, name="xc%d" % g0, align_bytes=256)
             nc.sync.dma_start(out=t[:].bitcast(I32), in_=x_words[g0:g1].rearrange("g p n -> p g n").bitcast(I32))
             for g in range(g0, g1):
                 x_code[g] = (t, g - g0)
 
         def load_w(c0, c1, g0, g1):
-            t = keep.tile([P, g1 - g0, 2 * COLS * (c1 - c0)], U8, name="wc%d_%d" % (c0, g0), align_bytes=64)
+            t = keep.tile([P, g1 - g0, 2 * COLS * (c1 - c0)], U8, name="wc%d_%d" % (c0, g0), align_bytes=256)
             nc.sync.dma_start(
                 out=t[:].bitcast(I32),
                 in_=w_words[g0:g1, :, 2 * COLS * c0 : 2 * COLS * c1].rearrange("g p n -> p g n").bitcast(I32),

@@ -230,7 +230,8 @@ def tile_ropeattention_pa_kernel(tc, x_words, x_scales, w_words, w_scales, w_bia
         for (c, i) in first:
             acc_of[(c, i)] = bank(4 * c + i, "acc%d_%d" % (c, i), COLS)
         for g in range(SPLIT):
-            for (c, i) in first:
+            order = first if g == 0 else [(c, i) for i in range(BLOCKS) for c in range(2)]
+            for (c, i) in order:
                 mx_pass(acc_of[(c, i)][:], c, i, g, 0, COLS)
 
         dst_of = {0: out_q, 1: out_k}

@@ -20,7 +20,7 @@ COLS = 512
 HALF = 128
 ROPE_BASE = 10000.0
 WARM = 4
-SPLIT = 3
+SPLIT = 2
 GROUP = 2
 
 
@@ -105,10 +105,10 @@ def tile_ropeattention_pa_kernel(tc, x_words, x_scales, w_words, w_scales, w_bia
         load_w(0, 2, 1, 2)
         load_planes(qs_c, w_scales, SPLIT, PASSES, 0, COLS)
         note_planes(qs_c, 0, 1, SPLIT, PASSES)
-        load_x(2, 3)
-        load_w(0, 2, 2, 3)
+        load_x(2, 4)
+        load_w(0, 1, 2, 4)
         load_planes(xs_b, x_scales, 4, PASSES, 0, COLS)
-        for (g0, g1) in ((3, 5), (5, 7), (7, 8)):
+        for (g0, g1) in ((4, 6), (6, 8)):
             load_x(g0, g1)
             load_w(0, 1, g0, g1)
 
@@ -151,7 +151,8 @@ def tile_ropeattention_pa_kernel(tc, x_words, x_scales, w_words, w_scales, w_bia
 
         load_planes(ks_b, w_scales, SPLIT, PASSES, COLS, COLS)
         note_planes(ks_b, 1, 2, SPLIT, PASSES)
-        load_w(1, 2, SPLIT, PASSES)
+        load_w(1, 2, SPLIT, 5)
+        load_w(1, 2, 5, PASSES)
         load_planes(vs, w_scales, 0, PASSES, 2 * COLS, COLS)
         note_planes(vs, 2, 3, 0, PASSES)
         load_w(2, 3, 0, 4)

@@ -21,6 +21,7 @@ HALF = 128
 ROPE_BASE = 10000.0
 WARM = 4
 SPLIT = 2
+Q_SHARED = 3
 GROUP = 2
 
 
@@ -234,6 +235,9 @@ def tile_ropeattention_pa_kernel(tc, x_words, x_scales, w_words, w_scales, w_bia
             order = first if g == 0 else [(c, i) for i in range(BLOCKS) for c in range(2)]
             for (c, i) in order:
                 mx_pass(acc_of[(c, i)][:], c, i, g, 0, COLS)
+        for g in range(SPLIT, Q_SHARED):
+            for i in range(BLOCKS):
+                mx_pass(acc_of[(0, i)][:], 0, i, g, 0, COLS)
 
         dst_of = {0: out_q, 1: out_k}
         bias_v = bias_sb[:, 2 * COLS : 3 * COLS]
@@ -266,7 +270,7 @@ def tile_ropeattention_pa_kernel(tc, x_words, x_scales, w_words, w_scales, w_bia
 
         for n0 in range(0, len(first), GROUP):
             group = range(n0, n0 + GROUP)
-            for g in range(SPLIT, PASSES):
+            for g in range(Q_SHARED if first[n0][0] == 0 else SPLIT, PASSES):
                 for n in group:
                     c, i = first[n]
                     mx_pass(acc_of[(c, i)][:], c, i, g, 0, COLS)

@@ -45,20 +45,16 @@ def tile_ropeattention_pa_kernel(tc, x_words, x_scales, w_words, w_scales, w_bia
             nc.vector.memset(pt[:].bitcast(I32), 0)
             return pt
 
-        brow = keep.tile([P, 768], BF16, name="brow")
-        nc.vector.memset(brow[:].bitcast(I32), 0)
-        nc.scalar.dma_start(out=brow[0:P:64, :], in_=w_bias.rearrange("(a n) -> a n", a=2))
-        sel = keep.tile([P, 2, P], BF16, name="sel")
-        nc.gpsimd.memset(sel[:].bitcast(F32), 0.0)
-        nc.gpsimd.memset(sel[0:1, 0, :], 1.0)
-        nc.gpsimd.memset(sel[64:65, 1, :], 1.0)
+        brow = keep.tile([P, 3 * COLS], BF16, name="brow")
+        nc.scalar.dma_start(out=brow[P - 1 : P, :], in_=w_bias.rearrange("(a n) -> a n", a=1))
+        warm = keep.tile([P, COLS], BF16, name="warm")
+        nc.gpsimd.memset(warm[:], 1.0)
         pos = keep.tile([P, 1], F32, name="pos")
         nc.gpsimd.iota(pos[:], pattern=[[0, 1]], base=0, channel_multiplier=1, allow_small_or_imprecise_dtypes=True)
 
-        warm = keep.tile([P, COLS], BF16, name="warm")
-        nc.vector.memset(warm[:].bitcast(I32), 0)
         xs_a = new_planes("xs_a", 0, 4, COLS)
         qks_a = new_planes("qks_a", 0, SPLIT, 2 * COLS)
+        nc.vector.memset(brow[0 : P - 1, :].bitcast(I32), 0)
         qs_c = new_planes("qs_c", SPLIT, PASSES, COLS)
         xs_b = new_planes("xs_b", 4, PASSES, COLS)
         x_plane = {}
@@ -163,17 +159,9 @@ def tile_ropeattention_pa_kernel(tc, x_words, x_scales, w_words, w_scales, w_bia
         for n in range(WARM):
             nc.tensor.matmul(out=warm_ps[:], lhsT=warm[:, 0:P], rhs=warm[:], start=True, stop=True)
         bias_sb = keep.tile([P, 3 * COLS], F32, name="bias_sb")
-        pieces = {0: [(0, 0, 0, 512)], 1: [(0, 512, 0, 256), (1, 0, 256, 256)], 2: [(1, 256, 0, 512)]}
         for c in range(3):
             b_ps = bank(5 + c, "bias_ps%d" % c, COLS)
-            for (row, src0, dst0, width) in pieces[c]:
-                nc.tensor.matmul(
-                    out=b_ps[:, dst0 : dst0 + width],
-                    lhsT=sel[:, row, :],
-                    rhs=brow[:, src0 : src0 + width],
-                    start=True,
-                    stop=True,
-                )
+            nc.tensor.matmul(out=b_ps[:], lhsT=warm[:, 0:P], rhs=brow[:, COLS * c : COLS * (c + 1)], start=True, stop=True)
             nc.scalar.copy(out=bias_sb[:, COLS * c : COLS * (c + 1)], in_=b_ps[:])
 
         tab = keep.tile([P, 2, 2, 2, HALF], F32, name="tab")

from contextlib import ExitStack
import math

import concourse.mybir as mybir

FLOPS = 2 * 512 * 4096 * 1536

F32 = mybir.dt.float32
BF16 = mybir.dt.bfloat16
I32 = mybir.dt.int32
U8 = mybir.dt.uint8
FP4X4 = mybir.dt.float4_e2m1fn_x4
ALU = mybir.AluOpType
ACTF = mybir.ActivationFunctionType

P = 128
PASSES = 8
BLOCKS = 4
COLS = 512
HALF = 128
ROPE_BASE = 10000.0
WARM = 4
SPLIT = 2
Q_SHARED = 3
GROUP = 2


def tile_ropeattention_pa_kernel(tc, x_words, x_scales, w_words, w_scales, w_bias, out_q, out_k, out_v):
    nc = tc.nc
    with ExitStack() as ctx:
        keep = ctx.enter_context(tc.tile_pool(name="keep", bufs=1))
        work = ctx.enter_context(tc.tile_pool(name="work", bufs=4))
        psum = ctx.enter_context(tc.psum_pool(name="psum", bufs=1))
        ctx.enter_context(tc.manual_schedule())

        x_code = {}
        w_code = {}
        w_plane = {}

        def bank(n, name, width):
            return psum.tile([P, width], F32, name=name, tag="bank%d" % n)

        def new_planes(name, g0, g1, width):
            pt = keep.tile([P, g1 - g0, width], U8, name=name, align_bytes=256)
            nc.vector.memset(pt[:].bitcast(I32), 0)
            return pt

        brow = keep.tile([P, 3 * COLS], BF16, name="brow")
        nc.scalar.dma_start(out=brow[P - 1 : P, :], in_=w_bias.rearrange("(a n) -> a n", a=1))
        warm = keep.tile([P, COLS], BF16, name="warm")
        nc.gpsimd.memset(warm[:], 1.0)
        pos = keep.tile([P, 1], F32, name="pos")
        nc.gpsimd.iota(pos[:], pattern=[[0, 1]], base=0, channel_multiplier=1, allow_small_or_imprecise_dtypes=True)

        xs_a = new_planes("xs_a", 0, 4, COLS)
        qks_a = new_planes("qks_a", 0, SPLIT, 2 * COLS)
        nc.vector.memset(brow[0 : P - 1, :].bitcast(I32), 0)
        qs_c = new_planes("qs_c", SPLIT, PASSES, COLS)
        xs_b = new_planes("xs_b", 4, PASSES, COLS)
        x_plane = {}
        for g in range(PASSES):
            x_plane[g] = (xs_a, g) if g < 4 else (xs_b, g - 4)

        scr = keep.tile([P, 1], F32, name="scr")
        nc.scalar.activation(out=scr[:], in_=warm[:, 0:1], func=ACTF.Sin)

        def load_planes(pt, src, g0, g1, c0, width):
            for r in range(4):
                nc.sync.dma_start(
                    out=pt[r : P : 32, :, :].bitcast(I32),
                    in_=src[g0:g1, r : 16 : 4, c0 : c0 + width].rearrange("g q n -> q g n").bitcast(I32),
                )

        def load_x(g0, g1):
            t = keep.tile([P, g1 - g0, 2 * COLS], U8, name="xc%d" % g0, align_bytes=256)
            nc.sync.dma_start(out=t[:].bitcast(I32), in_=x_words[g0:g1].rearrange("g p n -> p g n").bitcast(I32))
            for g in range(g0, g1):
                x_code[g] = (t, g - g0)

        def load_w(c0, c1, g0, g1):
            t = keep.tile([P, g1 - g0, 2 * COLS * (c1 - c0)], U8, name="wc%d_%d" % (c0, g0), align_bytes=256)
            nc.sync.dma_start(
                out=t[:].bitcast(I32),
                in_=w_words[g0:g1, :, 2 * COLS * c0 : 2 * COLS * c1].rearrange("g p n -> p g n").bitcast(I32),
            )
            for c in range(c0, c1):
                for g in range(g0, g1):
                    w_code[(c, g)] = (t, g - g0, COLS * (c - c0))

        def note_planes(pt, c0, c1, g0, g1):
            for c in range(c0, c1):
                for g in range(g0, g1):
                    w_plane[(c, g)] = (pt, g - g0, COLS * (c - c0))

        load_x(0, 1)
        load_w(0, 1, 0, 1)
        load_planes(xs_a, x_scales, 0, 4, 0, COLS)
        load_planes(qks_a, w_scales, 0, SPLIT, 0, 2 * COLS)
        note_planes(qks_a, 0, 2, 0, SPLIT)
        load_w(1, 2, 0, 1)
        load_x(1, 2)
        load_w(0, 2, 1, 2)
        load_planes(qs_c, w_scales, SPLIT, PASSES, 0, COLS)
        note_planes(qs_c, 0, 1, SPLIT, PASSES)
        load_x(2, 4)
        load_w(0, 1, 2, 4)
        load_planes(xs_b, x_scales, 4, PASSES, 0, COLS)
        for (g0, g1) in ((4, 6), (6, 8)):
            load_x(g0, g1)
            load_w(0, 1, g0, g1)

        inv = keep.tile([P, HALF], F32, name="inv")
        nc.vector.memset(inv[:, 0:1], 1.0)
        turn = keep.tile([P, 1], F32, name="turn")
        nc.vector.tensor_scalar(out=turn[:], in0=pos[:], scalar1=1.0 / (2.0 * math.pi), scalar2=None, op0=ALU.mult)
        for s in range(7):
            w = 2 ** s
            nc.vector.tensor_scalar(
                out=inv[:, w : 2 * w], in0=inv[:, 0:w], scalar1=ROPE_BASE ** (-w / 128.0), scalar2=None, op0=ALU.mult
            )
        ang = keep.tile([P, 4, HALF], F32, name="ang")
        for a in range(4):
            if a < 2:
                nc.vector.tensor_scalar(out=ang[:, a, :], in0=inv[:], scalar1=turn[:, 0:1], scalar2=None, op0=ALU.mult)
            else:
                nc.vector.tensor_scalar(
                    out=ang[:, a, :], in0=inv[:], scalar1=turn[:, 0:1], scalar2=0.25, op0=ALU.mult, op1=ALU.add
                )
        whole = keep.tile([P, 4, HALF], I32, name="whole")
        nc.vector.tensor_copy(out=whole[:], in_=ang[:])
        frac = keep.tile([P, 4, HALF], F32, name="frac")
        nc.vector.tensor_tensor(out=frac[:], in0=ang[:], in1=whole[:], op=ALU.subtract)
        nfr = keep.tile([P, 4, HALF], F32, name="nfr")
        nc.vector.scalar_tensor_tensor(
            out=nfr[:].rearrange("p a d -> p (a d)"),
            in0=frac[:].rearrange("p a d -> p (a d)"),
            scalar=0.5,
            in1=frac[:].rearrange("p a d -> p (a d)"),
            op0=ALU.is_gt,
            op1=ALU.subtract,
        )
        arg = keep.tile([P, 2, 2, HALF], F32, name="arg")
        nc.vector.tensor_copy(out=arg[:, 1, :, :], in_=nfr[:, 2:4, :])
        nc.vector.tensor_copy(out=arg[:, 0, 0, :], in_=nfr[:, 0, :])
        nc.vector.tensor_scalar(out=arg[:, 0, 1, :], in0=nfr[:, 1, :], scalar1=-1.0, scalar2=None, op0=ALU.mult)
        ks_b = new_planes("ks_b", SPLIT, PASSES, COLS)
        vs = new_planes("vs", 0, PASSES, COLS)

        load_planes(ks_b, w_scales, SPLIT, PASSES, COLS, COLS)
        note_planes(ks_b, 1, 2, SPLIT, PASSES)
        load_w(1, 2, SPLIT, 5)
        load_w(1, 2, 5, PASSES)
        load_planes(vs, w_scales, 0, PASSES, 2 * COLS, COLS)
        note_planes(vs, 2, 3, 0, PASSES)
        load_w(2, 3, 0, 4)
        load_w(2, 3, 4, 8)

        warm_ps = bank(4, "warm_ps", COLS)
        for n in range(WARM):
            nc.tensor.matmul(out=warm_ps[:], lhsT=warm[:, 0:P], rhs=warm[:], start=True, stop=True)
        bias_sb = keep.tile([P, 3 * COLS], F32, name="bias_sb")
        for c in range(3):
            b_ps = bank(5 + c, "bias_ps%d" % c, COLS)
            nc.tensor.matmul(out=b_ps[:], lhsT=warm[:, 0:P], rhs=brow[:, COLS * c : COLS * (c + 1)], start=True, stop=True)
            nc.scalar.copy(out=bias_sb[:, COLS * c : COLS * (c + 1)], in_=b_ps[:])

        tab = keep.tile([P, 2, 2, 2, HALF], F32, name="tab")
        for h in range(2):
            nc.scalar.activation(out=tab[:, :, h, :, :], in_=arg[:], func=ACTF.Sin, scale=-2.0 * math.pi)
        sin4 = tab[:, 0, :, :, :].rearrange("p h t d -> p (h t d)")
        cos4 = tab[:, 1, :, :, :].rearrange("p h t d -> p (h t d)")

        def products(eng, src, tag):
            mc = work.tile([P, COLS], F32, name="mc" + tag, tag="mc" + tag)
            ms = work.tile([P, COLS], F32, name="ms" + tag, tag="ms" + tag)
            eng.tensor_tensor(out=mc[:], in0=src, in1=cos4, op=ALU.mult)
            eng.tensor_tensor(out=ms[:], in0=src, in1=sin4, op=ALU.mult)
            return mc[:], ms[:]

        def both_products(src):
            m = work.tile([P, 2, COLS], F32, name="m2", tag="m2")
            nc.vector.tensor_tensor(
                out=m[:],
                in0=src.unsqueeze(1).to_broadcast([P, 2, COLS]),
                in1=tab[:].rearrange("p s h t d -> p s (h t d)"),
                op=ALU.mult,
            )
            return m[:, 1, :], m[:, 0, :]

        def combine(eng, pair, dst):
            mc, ms = pair
            eng.tensor_tensor(
                out=dst.rearrange("p (h t d) -> p h t d", h=2, t=2),
                in0=mc.rearrange("p (h t d) -> p h t d", h=2, t=2),
                in1=ms.rearrange("p (h t d) -> p h t d", h=2, t=2)[:, :, ::-1, :],
                op=ALU.add,
            )

        bias_rot = keep.tile([P, 2 * COLS], F32, name="bias_rot")
        combine(nc.gpsimd, products(nc.gpsimd, bias_sb[:, 0:COLS], "g"), bias_rot[:, 0:COLS])
        combine(nc.vector, products(nc.vector, bias_sb[:, COLS : 2 * COLS], ""), bias_rot[:, COLS : 2 * COLS])

        def mx_pass(acc, c, i, g, n0, n1):
            xt, xl = x_code[g]
            xp, xpl = x_plane[g]
            wt, wl, wo = w_code[(c, g)]
            st, sl, so = w_plane[(c, g)]
            nc.tensor.matmul_mx(
                out=acc,
                lhsT=xt[:, xl, 2 * P * i : 2 * P * (i + 1)].bitcast(FP4X4),
                lhsT_scale=xp[:, xpl, P * i : P * (i + 1)],
                rhs=wt[:, wl, 2 * (wo + n0) : 2 * (wo + n1)].bitcast(FP4X4),
                rhs_scale=st[:, sl, so + n0 : so + n1],
                start=(g == 0),
                stop=(g == PASSES - 1),
            )

        first = [(c, i) for c in range(2) for i in range(BLOCKS)]
        acc_of = {}
        for (c, i) in first:
            acc_of[(c, i)] = bank(4 * c + i, "acc%d_%d" % (c, i), COLS)
        for g in range(SPLIT):
            order = first if g == 0 else [(c, i) for i in range(BLOCKS) for c in range(2)]
            for (c, i) in order:
                mx_pass(acc_of[(c, i)][:], c, i, g, 0, COLS)
        for g in range(SPLIT, Q_SHARED):
            for i in range(BLOCKS):
                mx_pass(acc_of[(0, i)][:], 0, i, g, 0, COLS)

        dst_of = {0: out_q, 1: out_k}
        bias_v = bias_sb[:, 2 * COLS : 3 * COLS]

        def add_on_gpsimd(name, src, addend, dst):
            o = keep.tile([P, COLS], F32, name=name)
            nc.gpsimd.tensor_tensor(out=o[:], in0=src, in1=addend, op=ALU.add)
            nc.sync.dma_start(out=dst.rearrange("h l d -> l h d"), in_=o[:].rearrange("p (h e) -> p h e", h=2))

        rots = {}

        def bias_rope(n):
            c, i = first[n]
            add_on_gpsimd("o_rope%d" % n, rots[n][:], bias_rot[:, COLS * c : COLS * (c + 1)], dst_of[c][i])

        def finish(n, pair):
            rot = keep.tile([P, COLS], F32, name="rot%d" % n)
            combine(nc.vector, pair, rot[:])
            rots[n] = rot
            if n < len(first) - 1:
                bias_rope(n)

        def v_tile(i):
            acc = bank(i, "acc2_%d" % i, COLS)
            for g in range(PASSES):
                mx_pass(acc[:], 2, i, g, 0, COLS)
            o = keep.tile([P, COLS], F32, name="o_v%d" % i)
            nc.vector.tensor_tensor(out=o[:], in0=acc[:], in1=bias_v, op=ALU.add)
            nc.scalar.dma_start(out=out_v[i].rearrange("h l d -> l h d"), in_=o[:].rearrange("p (h e) -> p h e", h=2))

        for n0 in range(0, len(first), GROUP):
            group = range(n0, n0 + GROUP)
            for g in range(Q_SHARED if first[n0][0] == 0 else SPLIT, PASSES):
                for n in group:
                    c, i = first[n]
                    mx_pass(acc_of[(c, i)][:], c, i, g, 0, COLS)
            held = {}
            for n in group:
                held[n] = both_products(acc_of[first[n]][:])
            if n0 + GROUP == len(first):
                v_tile(0)
            for n in group:
                finish(n, held[n])

        for i in (1, 2):
            v_tile(i)
        c7, i7 = first[-1]
        o7 = keep.tile([P, COLS], F32, name="o_rope7")
        nc.vector.tensor_tensor(out=o7[:], in0=rots[7][:], in1=bias_rot[:, COLS * c7 : COLS * (c7 + 1)], op=ALU.add)
        nc.sync.dma_start(out=dst_of[c7][i7].rearrange("h l d -> l h d"), in_=o7[:].rearrange("p (h e) -> p h e", h=2))

        i = BLOCKS - 1
        for h in range(2):
            acc = bank(3 + h, "acc2_3%d" % h, COLS // 2)
            for g in range(PASSES):
                mx_pass(acc[:], 2, i, g, 256 * h, 256 * (h + 1))
            o = keep.tile([P, COLS // 2], F32, name="o_v3%d" % h)
            nc.vector.tensor_tensor(out=o[:], in0=acc[:], in1=bias_v[:, 256 * h : 256 * (h + 1)], op=ALU.add)
            nc.scalar.dma_start(out=out_v[i, h], in_=o[:])
